import numpy as np
import ml_dtypes


def mxq(x, axis, fmt="e4m3"):
    dtype, down = {"e4m3": (ml_dtypes.float8_e4m3fn, 7), "e5m2": (ml_dtypes.float8_e5m2, 14)}[fmt]
    v = np.moveaxis(np.asarray(x, np.float32).astype(ml_dtypes.bfloat16).astype(np.float64), axis, -1)
    blocks = v.reshape(v.shape[:-1] + (-1, 32))
    amax = np.abs(blocks).max(-1, keepdims=True)
    byte = np.maximum(np.where(amax > 0, np.frexp(amax)[1] - 1 + 127, 0) - down, 1)
    scale = np.exp2(byte - 127.0)
    codes = (blocks / scale).astype(np.float32).astype(dtype).astype(np.float64)
    return np.moveaxis((codes * scale).reshape(v.shape), -1, axis)


WIDE = False


def mx_kscale(k):
    if not WIDE:
        return np.ones(k)
    levels = np.array([30, -30])
    if k % 512:
        return np.exp2(np.random.permutation(np.resize(levels, k // 32))).repeat(32)
    a = np.empty((k // 512, 16))
    for p in range(k // 512):
        a[p, :8] = np.random.permutation(np.resize(levels, 8))
        for g in range(8):
            far = levels[np.abs(levels - a[p, g]) >= 10]
            a[p, g + 8] = far[np.random.randint(len(far))]
    return np.exp2(a.ravel()).repeat(32)


BF16 = ml_dtypes.bfloat16


def bf(x):
    return np.asarray(x, np.float32).astype(BF16)


def f64(x):
    return np.asarray(x).astype(np.float64)


B, S, H, NH, NKV, HD = 2, 512, 2048, 16, 4, 128
EPS = 1e-6


def rms_norm(x, w):
    var = np.mean(x * x, axis=-1, keepdims=True)
    return x * (1.0 / np.sqrt(var + EPS)) * w


def rotate_half(x):
    x1, x2 = np.split(x, 2, axis=-1)
    return np.concatenate([-x2, x1], axis=-1)


def setup_inputs():
    s = mx_kscale(H)
    inv_freq = 1.0 / (10000.0 ** (np.arange(0, HD, 2) / HD))
    freqs = np.arange(S)[:, None] * inv_freq[None, :]
    emb = np.concatenate([freqs, freqs], axis=-1)
    return {"hidden_states": bf(np.random.standard_normal((B, S, H)) * s),
            "cos": bf(np.cos(emb)),
            "sin": bf(np.sin(emb)),
            "wq": bf(np.random.standard_normal((NH * HD, H)) / np.sqrt(H) / s[None, :]),
            "wk": bf(np.random.standard_normal((NKV * HD, H)) / np.sqrt(H) / s[None, :]),
            "q_norm_w": bf(1.0 + 0.1 * np.random.standard_normal(HD)),
            "k_norm_w": bf(1.0 + 0.1 * np.random.standard_normal(HD)),
            "ssmax_scale": bf((1.0 + 0.2 * np.random.standard_normal((1, NH, 1, 1))) / np.log(S))}


def reference(hidden_states, cos, sin, wq, wk, q_norm_w, k_norm_w, ssmax_scale):
    xq = mxq(f64(hidden_states), 2, "e5m2")
    q = (xq @ mxq(f64(wq), 1, "e5m2").T).reshape(B, S, NH, HD)
    k = (xq @ mxq(f64(wk), 1, "e5m2").T).reshape(B, S, NKV, HD)
    q = rms_norm(q, f64(q_norm_w)).transpose(0, 2, 1, 3)
    k = rms_norm(k, f64(k_norm_w)).transpose(0, 2, 1, 3)
    c = f64(cos)[None, None]
    sn = f64(sin)[None, None]
    q = q * c + rotate_half(q) * sn
    k = k * c + rotate_half(k) * sn
    q = q * (f64(ssmax_scale) * np.log(S))
    return q, k

@@ -1,0 +1,305 @@
+import math
+from contextlib import ExitStack
+
+import concourse.mybir as mybir
+from concourse.masks import make_identity
+
+B, S, H, NH, NKV, HD = 2, 512, 2048, 16, 4, 128
+EPS = 1e-6
+FLOPS = 2 * B * S * H * (NH + NKV) * HD
+
+F32 = mybir.dt.float32
+BF16 = mybir.dt.bfloat16
+U32 = mybir.dt.uint32
+U8 = mybir.dt.uint8
+E5X4 = mybir.dt.float8_e5m2_x4
+MULT = mybir.AluOpType.mult
+ADD = mybir.AluOpType.add
+ACT = mybir.ActivationFunctionType
+
+P = 128
+PASSES = H // 512
+JT = S // P
+TT = B * JT
+HPB = 4
+NT = (NH + NKV) // HPB
+NQ = NH // HPB
+HALF = HD // 2
+
+def units_after():
+    table = {}
+    table[0] = [("x", 4)]
+    table[1] = [("x", 5)]
+    table[2] = [("x", 6)]
+    table[3] = [("x", 7)]
+    table[4] = [("w", 1, 0), ("w", 1, 1)]
+    table[5] = [("w", 1, 2), ("w", 1, 3)]
+    for n in range(1, NT - 1):
+        table[n * TT + 0] = [("w", n + 1, 0)]
+        table[n * TT + 2] = [("w", n + 1, 1)]
+        table[n * TT + 4] = [("w", n + 1, 2)]
+        table[n * TT + 5] = [("w", n + 1, 3)]
+    return table
+
+
+def tile_biboattention_pa_kernel(
+    tc, hidden_states, cos, sin, wq, wk, q_norm_w, k_norm_w, ssmax_scale, out_0, out_1
+):
+    nc = tc.nc
+    with ExitStack() as ctx:
+        keep = ctx.enter_context(tc.tile_pool(name="keep", bufs=1))
+        wraw_pool = ctx.enter_context(tc.tile_pool(name="wraw", bufs=3))
+        wcode_pool = ctx.enter_context(tc.tile_pool(name="wcode", bufs=2))
+        grp_pool = ctx.enter_context(tc.tile_pool(name="grp", bufs=4))
+        stat_pool = ctx.enter_context(tc.tile_pool(name="stat", bufs=4))
+        rope_pool = ctx.enter_context(tc.tile_pool(name="rope", bufs=3))
+        out_pool = ctx.enter_context(tc.tile_pool(name="outp", bufs=3))
+        acc_pool = ctx.enter_context(tc.psum_pool(name="accp", bufs=4))
+        tp_pool = ctx.enter_context(tc.psum_pool(name="tpp", bufs=4))
+        ctx.enter_context(tc.manual_schedule())
+
+        ident = keep.tile([P, P], F32, name="ident", tag="ident")
+        make_identity(nc, ident[:])
+        ones = keep.tile([P, P], BF16, name="ones", tag="ones")
+        nc.gpsimd.memset(ones[:], 1.0)
+        vec_row = keep.tile([P, 272], BF16, name="vec_row", tag="vec_row")
+        nc.gpsimd.memset(vec_row[:], 0.0)
+        gain = keep.tile([P, NH + NKV], F32, name="gain", tag="gain")
+        nc.gpsimd.memset(gain[:, NH : NH + NKV], 1.0)
+        warm = keep.tile([P, 1], F32, name="warm", tag="warm")
+        nc.vector.memset(warm[:], 1.0)
+        warm_out = keep.tile([P, 1], F32, name="warm_out", tag="warm_out")
+        junk = keep.tile([P, HD], F32, name="junk", tag="junk")
+
+        cos_sb = keep.tile([P, JT, HD], BF16, name="cos_sb", tag="cos_sb")
+        sin_sb = keep.tile([P, JT, HD], BF16, name="sin_sb", tag="sin_sb")
+        nc.scalar.dma_start(out=cos_sb[:], in_=cos.rearrange("(p j) d -> p j d", j=JT))
+        nc.scalar.dma_start(out=sin_sb[:], in_=sin.rearrange("(p j) d -> p j d", j=JT))
+        nc.scalar.activation(out=warm_out[:], in_=warm[:], func=ACT.Sqrt)
+        nc.scalar.dma_start(out=vec_row[0:1, 0:HD], in_=q_norm_w.rearrange("(o d) -> o d", o=1))
+        nc.scalar.dma_start(out=vec_row[0:1, HD : 2 * HD], in_=k_norm_w.rearrange("(o d) -> o d", o=1))
+        nc.scalar.dma_start(
+            out=vec_row[0:1, 2 * HD : 2 * HD + NH], in_=ssmax_scale.rearrange("a h b c -> a (h b c)")
+        )
+
+        x_raw = []
+        for b in range(B):
+            x_raw.append(keep.tile([P, JT, H], BF16, name="x_raw%d" % b, tag="x_raw%d" % b))
+        w_raw = {}
+
+        def load_x(b):
+            src = hidden_states[b].rearrange("(p j) k -> p j k", j=JT)
+            for j in range(JT):
+                nc.sync.dma_start(out=x_raw[b][:, j, :], in_=src[:, j, :])
+
+        def load_w(n):
+            w_raw[n] = wraw_pool.tile([P, HPB, H], BF16, name="w_raw", tag="w_raw")
+            for r in range(HPB):
+                if n < NQ:
+                    rows = wq[(n * HPB + r) * P : (n * HPB + r + 1) * P, :]
+                else:
+                    rows = wk[r * P : (r + 1) * P, :]
+                nc.sync.dma_start(out=w_raw[n][:, r, :], in_=rows)
+
+        load_x(0)
+        load_w(0)
+        load_x(1)
+        load_w(1)
+        load_w(2)
+
+        x_codes = keep.tile([P, TT, PASSES, P], U32, name="x_codes", tag="x_codes", align_bytes=64)
+        x_scales = keep.tile([P, TT, PASSES, P], U8, name="x_scales", tag="x_scales", align_bytes=64)
+        w_codes = {}
+        w_scales = {}
+        tables = {}
+
+        def transposes(words):
+            banks = []
+            for half in range(2):
+                tp = tp_pool.tile([P, 512], F32, name="tp", tag="tp")
+                for gg in range(2):
+                    g = 2 * half + gg
+                    for u in range(2):
+                        c = 2 * gg + u
+                        nc.tensor.transpose(
+                            tp[:, c * P : (c + 1) * P], words[:, 256 * g + u : 256 * (g + 1) : 2], ident[:]
+                        )
+                banks.append(tp)
+            return banks
+
+        def interleave(banks):
+            grouped = grp_pool.tile([P, PASSES, P, 4], BF16, name="grouped", tag="grouped", align_bytes=64)
+            gwords = grouped[:].bitcast(F32)
+            for half in range(2):
+                nc.scalar.copy(
+                    out=gwords[:, 2 * half : 2 * half + 2, :, :],
+                    in_=banks[half][:].rearrange("p (g u r) -> p g r u", g=2, u=2),
+                )
+            return grouped
+
+        def quantize(unit, grouped):
+            if unit[0] == "x":
+                tt = unit[1]
+                nc.vector.quantize_mx(
+                    out=x_codes[:, tt, :, :].rearrange("p g r -> p (g r)").bitcast(E5X4),
+                    scales=x_scales[:, tt, :, :].rearrange("p g r -> p (g r)"),
+                    in_=grouped[:].rearrange("p g r t -> p (g r t)"),
+                )
+            else:
+                n, r = unit[1], unit[2]
+                for g in range(PASSES):
+                    nc.vector.quantize_mx(
+                        out=w_codes[n][:, g, r * P : (r + 1) * P].bitcast(E5X4),
+                        scales=w_scales[n][:, g, r * P : (r + 1) * P],
+                        in_=grouped[:, g, :, :].rearrange("p r t -> p (r t)"),
+                    )
+
+        def prepare(unit):
+            if unit[0] == "x":
+                tt = unit[1]
+                words = x_raw[tt // JT][:, tt % JT, :].bitcast(F32)
+            else:
+                n, r = unit[1], unit[2]
+                if r == 0:
+                    w_codes[n] = wcode_pool.tile(
+                        [P, PASSES, 512], U32, name="w_codes", tag="w_codes", align_bytes=64
+                    )
+                    w_scales[n] = wcode_pool.tile(
+                        [P, PASSES, 512], U8, name="w_scales", tag="w_scales", align_bytes=64
+                    )
+                words = w_raw[n][:, r, :].bitcast(F32)
+            banks = transposes(words)
+            if unit[0] == "w" and unit[2] == HPB - 1 and unit[1] + 3 < NT:
+                load_w(unit[1] + 3)
+            return (unit, interleave(banks))
+
+        def build_tables():
+            cb = tp_pool.tile([P, 512], F32, name="cb", tag="tp")
+            nc.tensor.matmul(out=cb[:, 0:272], lhsT=ones[:], rhs=vec_row[:], start=True, stop=True)
+            for which in range(2):
+                w0 = which * HD
+                tab = keep.tile([P, JT, 2, HD], F32, name="tab%d" % which, tag="tab%d" % which)
+                tables[which] = tab
+                nc.vector.tensor_tensor(
+                    out=tab[:, :, 0, :],
+                    in0=cos_sb[:],
+                    in1=cb[:, w0 : w0 + HD].unsqueeze(1).to_broadcast([P, JT, HD]),
+                    op=MULT,
+                )
+                nc.vector.tensor_tensor(
+                    out=tab[:, :, 1, 0:HALF],
+                    in0=sin_sb[:, :, HALF:HD],
+                    in1=cb[:, w0 : w0 + HALF].unsqueeze(1).to_broadcast([P, JT, HALF]),
+                    op=MULT,
+                )
+                nc.vector.scalar_tensor_tensor(
+                    out=tab[:, :, 1, HALF:HD],
+                    in0=sin_sb[:, :, 0:HALF],
+                    scalar=-1.0,
+                    in1=cb[:, w0 + HALF : w0 + HD].unsqueeze(1).to_broadcast([P, JT, HALF]),
+                    op0=MULT,
+                    op1=MULT,
+                )
+            nc.vector.tensor_scalar(
+                out=gain[:, 0:NH], in0=cb[:, 2 * HD : 2 * HD + NH], scalar1=math.log(S), scalar2=None, op0=MULT
+            )
+
+        def project(n, tt):
+            acc = acc_pool.tile([P, 512], F32, name="acc", tag="acc")
+            for g in range(PASSES):
+                nc.tensor.matmul_mx(
+                    out=acc[:],
+                    lhsT=x_codes[:, tt, g, :].bitcast(E5X4),
+                    lhsT_scale=x_scales[:, tt, g, :],
+                    rhs=w_codes[n][:, g, :].bitcast(E5X4),
+                    rhs_scale=w_scales[n][:, g, :],
+                    start=(g == 0),
+                    stop=(g == PASSES - 1),
+                )
+            return acc
+
+        def root_mean_square(acc):
+            ss = stat_pool.tile([P, HPB], F32, name="ss", tag="ss")
+            for h in range(HPB):
+                nc.scalar.activation(
+                    out=junk[:], in_=acc[:, h * HD : (h + 1) * HD], func=ACT.Square, accum_out=ss[:, h : h + 1]
+                )
+            rms = stat_pool.tile([P, HPB], F32, name="rms", tag="rms")
+            nc.scalar.activation(out=rms[:], in_=ss[:], func=ACT.Sqrt, scale=1.0 / HD, bias=EPS)
+            return rms
+
+        def rope_head(blk, h):
+            nc.vector.scalar_tensor_tensor(
+                out=blk["t12"][:, h, :, :],
+                in0=blk["acc"][:, h * HD : (h + 1) * HD].unsqueeze(1).to_broadcast([P, 2, HD]),
+                scalar=blk["rg"][:, h : h + 1],
+                in1=tables[0 if blk["n"] < NQ else 1][:, blk["tt"] % JT, :, :],
+                op0=MULT,
+                op1=MULT,
+            )
+
+        out_tiles = {}
+
+        def finish(blk):
+            n, tt = blk["n"], blk["tt"]
+            b, j = tt // JT, tt % JT
+            if j == 0:
+                out_tiles[0] = out_pool.tile([P, HPB, JT, HD], F32, name="o_t", tag="o_t")
+            o_t = out_tiles[0]
+            t12 = blk["t12"]
+            nc.gpsimd.tensor_tensor(
+                out=o_t[:, :, j, 0:HALF], in0=t12[:, :, 0, 0:HALF], in1=t12[:, :, 1, HALF:HD], op=ADD
+            )
+            nc.gpsimd.tensor_tensor(
+                out=o_t[:, :, j, HALF:HD], in0=t12[:, :, 0, HALF:HD], in1=t12[:, :, 1, 0:HALF], op=ADD
+            )
+            if j == JT - 1:
+                if n < NQ:
+                    dst = out_0[b, n * HPB : (n + 1) * HPB]
+                else:
+                    dst = out_1[b]
+                nc.sync.dma_start(
+                    out=dst.rearrange("h (p j) d -> p h (j d)", j=JT),
+                    in_=o_t[:].rearrange("p h j d -> p h (j d)"),
+                )
+
+        head = [("x", 0), ("x", 1), ("x", 2), ("x", 3), ("w", 0, 0), ("w", 0, 1), ("w", 0, 2), ("w", 0, 3)]
+        for i, unit in enumerate(head):
+            done = prepare(unit)
+            quantize(done[0], done[1])
+            if i == 1:
+                build_tables()
+
+        after = units_after()
+        waiting = []
+        prev = None
+        for m in range(NT * TT):
+            n, tt = m // TT, m % TT
+            blk = {"n": n, "tt": tt}
+            blk["acc"] = project(n, tt)
+            rms = root_mean_square(blk["acc"])
+            if prev is not None:
+                prev["t12"] = rope_pool.tile([P, HPB, 2, HD], F32, name="t12", tag="t12")
+                rope_head(prev, 0)
+                rope_head(prev, 1)
+            for done in waiting:
+                quantize(done[0], done[1])
+            waiting = []
+            rinv = stat_pool.tile([P, HPB], F32, name="rinv", tag="rinv")
+            nc.vector.reciprocal(out=rinv[:], in_=rms[:])
+            if prev is not None:
+                rope_head(prev, 2)
+            blk["rg"] = stat_pool.tile([P, HPB], F32, name="rg", tag="rg")
+            nc.vector.tensor_tensor(
+                out=blk["rg"][:], in0=rinv[:], in1=gain[:, n * HPB : (n + 1) * HPB], op=MULT
+            )
+            if prev is not None:
+                rope_head(prev, 3)
+                finish(prev)
+            for unit in after.get(m, []):
+                waiting.append(prepare(unit))
+            prev = blk
+        prev["t12"] = rope_pool.tile([P, HPB, 2, HD], F32, name="t12", tag="t12")
+        for h in range(HPB):
+            rope_head(prev, h)
+        finish(prev)

@@ -25,20 +25,20 @@ HPB = 4
 NT = (NH + NKV) // HPB
 NQ = NH // HPB
 HALF = HD // 2
+ADD_ON_GPSIMD = True
+RSQRT = True
+
 
 def units_after():
     table = {}
-    table[0] = [("x", 4)]
-    table[1] = [("x", 5)]
-    table[2] = [("x", 6)]
-    table[3] = [("x", 7)]
-    table[4] = [("w", 1, 0), ("w", 1, 1)]
-    table[5] = [("w", 1, 2), ("w", 1, 3)]
+    table[0] = [("x", 2), ("x", 3)]
+    table[1] = [("w", 1, 0), ("w", 1, 1)]
+    table[2] = [("x", 4), ("x", 5)]
+    table[3] = [("w", 1, 2), ("w", 1, 3)]
+    table[4] = [("x", 6), ("x", 7)]
     for n in range(1, NT - 1):
-        table[n * TT + 0] = [("w", n + 1, 0)]
-        table[n * TT + 2] = [("w", n + 1, 1)]
-        table[n * TT + 4] = [("w", n + 1, 2)]
-        table[n * TT + 5] = [("w", n + 1, 3)]
+        table[n * TT + 1] = [("w", n + 1, 0), ("w", n + 1, 1)]
+        table[n * TT + 3] = [("w", n + 1, 2), ("w", n + 1, 3)]
     return table
 
 
@@ -50,22 +50,22 @@ def tile_biboattention_pa_kernel(
         keep = ctx.enter_context(tc.tile_pool(name="keep", bufs=1))
         wraw_pool = ctx.enter_context(tc.tile_pool(name="wraw", bufs=3))
         wcode_pool = ctx.enter_context(tc.tile_pool(name="wcode", bufs=2))
-        grp_pool = ctx.enter_context(tc.tile_pool(name="grp", bufs=4))
+        grpw_pool = ctx.enter_context(tc.tile_pool(name="grpw", bufs=2))
+        grpx_pool = ctx.enter_context(tc.tile_pool(name="grpx", bufs=3))
         stat_pool = ctx.enter_context(tc.tile_pool(name="stat", bufs=4))
         rope_pool = ctx.enter_context(tc.tile_pool(name="rope", bufs=3))
         out_pool = ctx.enter_context(tc.tile_pool(name="outp", bufs=3))
+        const_psum = ctx.enter_context(tc.psum_pool(name="constp", bufs=1))
         acc_pool = ctx.enter_context(tc.psum_pool(name="accp", bufs=4))
-        tp_pool = ctx.enter_context(tc.psum_pool(name="tpp", bufs=4))
+        tp_pool = ctx.enter_context(tc.psum_pool(name="tpp", bufs=3))
         ctx.enter_context(tc.manual_schedule())
 
+        vec_row = keep.tile([P, 272], BF16, name="vec_row", tag="vec_row")
+        nc.gpsimd.memset(vec_row[:], 0.0)
         ident = keep.tile([P, P], F32, name="ident", tag="ident")
         make_identity(nc, ident[:])
         ones = keep.tile([P, P], BF16, name="ones", tag="ones")
         nc.gpsimd.memset(ones[:], 1.0)
-        vec_row = keep.tile([P, 272], BF16, name="vec_row", tag="vec_row")
-        nc.gpsimd.memset(vec_row[:], 0.0)
-        gain = keep.tile([P, NH + NKV], F32, name="gain", tag="gain")
-        nc.gpsimd.memset(gain[:, NH : NH + NKV], 1.0)
         warm = keep.tile([P, 1], F32, name="warm", tag="warm")
         nc.vector.memset(warm[:], 1.0)
         warm_out = keep.tile([P, 1], F32, name="warm_out", tag="warm_out")
@@ -73,13 +73,15 @@ def tile_biboattention_pa_kernel(
 
         cos_sb = keep.tile([P, JT, HD], BF16, name="cos_sb", tag="cos_sb")
         sin_sb = keep.tile([P, JT, HD], BF16, name="sin_sb", tag="sin_sb")
-        nc.scalar.dma_start(out=cos_sb[:], in_=cos.rearrange("(p j) d -> p j d", j=JT))
-        nc.scalar.dma_start(out=sin_sb[:], in_=sin.rearrange("(p j) d -> p j d", j=JT))
-        nc.scalar.activation(out=warm_out[:], in_=warm[:], func=ACT.Sqrt)
         nc.scalar.dma_start(out=vec_row[0:1, 0:HD], in_=q_norm_w.rearrange("(o d) -> o d", o=1))
         nc.scalar.dma_start(out=vec_row[0:1, HD : 2 * HD], in_=k_norm_w.rearrange("(o d) -> o d", o=1))
         nc.scalar.dma_start(
             out=vec_row[0:1, 2 * HD : 2 * HD + NH], in_=ssmax_scale.rearrange("a h b c -> a (h b c)")
+        )
+        nc.scalar.dma_start(out=cos_sb[:], in_=cos.rearrange("(p j) d -> p j d", j=JT))
+        nc.scalar.dma_start(out=sin_sb[:], in_=sin.rearrange("(p j) d -> p j d", j=JT))
+        nc.scalar.activation(
+            out=warm_out[:], in_=warm[:], func=(ACT.Abs_reciprocal_sqrt if RSQRT else ACT.Sqrt)
         )
 
         x_raw = []
@@ -87,31 +89,41 @@ def tile_biboattention_pa_kernel(
             x_raw.append(keep.tile([P, JT, H], BF16, name="x_raw%d" % b, tag="x_raw%d" % b))
         w_raw = {}
 
-        def load_x(b):
-            src = hidden_states[b].rearrange("(p j) k -> p j k", j=JT)
-            for j in range(JT):
-                nc.sync.dma_start(out=x_raw[b][:, j, :], in_=src[:, j, :])
+        def load_x(tt):
+            src = hidden_states[tt // JT].rearrange("(p j) k -> p j k", j=JT)
+            nc.sync.dma_start(out=x_raw[tt // JT][:, tt % JT, :], in_=src[:, tt % JT, :])
 
-        def load_w(n):
-            w_raw[n] = wraw_pool.tile([P, HPB, H], BF16, name="w_raw", tag="w_raw")
-            for r in range(HPB):
-                if n < NQ:
-                    rows = wq[(n * HPB + r) * P : (n * HPB + r + 1) * P, :]
-                else:
-                    rows = wk[r * P : (r + 1) * P, :]
-                nc.sync.dma_start(out=w_raw[n][:, r, :], in_=rows)
+        def load_w(n, r):
+            if r == 0:
+                w_raw[n] = wraw_pool.tile([P, HPB, H], BF16, name="w_raw", tag="w_raw")
+            if n < NQ:
+                rows = wq[(n * HPB + r) * P : (n * HPB + r + 1) * P, :]
+            else:
+                rows = wk[r * P : (r + 1) * P, :]
+            nc.sync.dma_start(out=w_raw[n][:, r, :], in_=rows)
 
-        load_x(0)
-        load_w(0)
-        load_x(1)
-        load_w(1)
-        load_w(2)
+        for r in range(HPB):
+            load_w(0, r)
+        for tt in range(4):
+            load_x(tt)
+        load_w(1, 0)
+        load_w(1, 1)
+        load_x(4)
+        load_x(5)
+        load_w(1, 2)
+        load_w(1, 3)
+        load_x(6)
+        load_x(7)
+        for r in range(HPB):
+            load_w(2, r)
 
         x_codes = keep.tile([P, TT, PASSES, P], U32, name="x_codes", tag="x_codes", align_bytes=64)
         x_scales = keep.tile([P, TT, PASSES, P], U8, name="x_scales", tag="x_scales", align_bytes=64)
         w_codes = {}
         w_scales = {}
+        w_grouped = {}
         tables = {}
+        vcopy = []
 
         def transposes(words):
             banks = []
@@ -127,37 +139,35 @@ def tile_biboattention_pa_kernel(
                 banks.append(tp)
             return banks
 
-        def interleave(banks):
-            grouped = grp_pool.tile([P, PASSES, P, 4], BF16, name="grouped", tag="grouped", align_bytes=64)
-            gwords = grouped[:].bitcast(F32)
-            for half in range(2):
-                nc.scalar.copy(
-                    out=gwords[:, 2 * half : 2 * half + 2, :, :],
-                    in_=banks[half][:].rearrange("p (g u r) -> p g r u", g=2, u=2),
-                )
-            return grouped
+        def quantize_x(tt, grouped):
+            nc.vector.quantize_mx(
+                out=x_codes[:, tt, :, :].rearrange("p g r -> p (g r)").bitcast(E5X4),
+                scales=x_scales[:, tt, :, :].rearrange("p g r -> p (g r)"),
+                in_=grouped[:].rearrange("p g r t -> p (g r t)"),
+            )
 
-        def quantize(unit, grouped):
-            if unit[0] == "x":
-                tt = unit[1]
+        def quantize_w_tile(n, r):
+            for g in range(PASSES):
                 nc.vector.quantize_mx(
-                    out=x_codes[:, tt, :, :].rearrange("p g r -> p (g r)").bitcast(E5X4),
-                    scales=x_scales[:, tt, :, :].rearrange("p g r -> p (g r)"),
-                    in_=grouped[:].rearrange("p g r t -> p (g r t)"),
+                    out=w_codes[n][:, g, r * P : (r + 1) * P].bitcast(E5X4),
+                    scales=w_scales[n][:, g, r * P : (r + 1) * P],
+                    in_=w_grouped[n][:, g, r, :, :].rearrange("p r t -> p (r t)"),
                 )
-            else:
-                n, r = unit[1], unit[2]
-                for g in range(PASSES):
-                    nc.vector.quantize_mx(
-                        out=w_codes[n][:, g, r * P : (r + 1) * P].bitcast(E5X4),
-                        scales=w_scales[n][:, g, r * P : (r + 1) * P],
-                        in_=grouped[:, g, :, :].rearrange("p r t -> p (r t)"),
-                    )
+
+        def quantize_w_passes(n, c):
+            nc.vector.quantize_mx(
+                out=w_codes[n][:, 2 * c : 2 * c + 2, :].rearrange("p g c -> p (g c)").bitcast(E5X4),
+                scales=w_scales[n][:, 2 * c : 2 * c + 2, :].rearrange("p g c -> p (g c)"),
+                in_=w_grouped[n][:, 2 * c : 2 * c + 2, :, :, :].rearrange("p g h r t -> p (g h r t)"),
+            )
 
         def prepare(unit):
             if unit[0] == "x":
                 tt = unit[1]
                 words = x_raw[tt // JT][:, tt % JT, :].bitcast(F32)
+                grouped = grpx_pool.tile([P, PASSES, P, 4], BF16, name="x_grouped", tag="x_grouped", align_bytes=64)
+                gwords = grouped[:].bitcast(F32)
+                due = [lambda: quantize_x(tt, grouped)]
             else:
                 n, r = unit[1], unit[2]
                 if r == 0:
@@ -167,42 +177,63 @@ def tile_biboattention_pa_kernel(
                     w_scales[n] = wcode_pool.tile(
                         [P, PASSES, 512], U8, name="w_scales", tag="w_scales", align_bytes=64
                     )
+                    w_grouped[n] = grpw_pool.tile(
+                        [P, PASSES, HPB, P, 4], BF16, name="w_grouped", tag="w_grouped", align_bytes=64
+                    )
                 words = w_raw[n][:, r, :].bitcast(F32)
+                gwords = w_grouped[n][:].bitcast(F32)[:, :, r, :, :]
+                if n == 0:
+                    due = [lambda: quantize_w_tile(n, r)]
+                elif r == HPB - 1:
+                    due = [lambda: quantize_w_passes(n, 0), lambda: quantize_w_passes(n, 1)]
+                else:
+                    due = []
             banks = transposes(words)
             if unit[0] == "w" and unit[2] == HPB - 1 and unit[1] + 3 < NT:
-                load_w(unit[1] + 3)
-            return (unit, interleave(banks))
+                for row in range(HPB):
+                    load_w(unit[1] + 3, row)
+            for half in range(2):
+                dst = gwords[:, 2 * half : 2 * half + 2, :, :]
+                src = banks[half][:].rearrange("p (g u r) -> p g r u", g=2, u=2)
+                if (unit[0], half) in vcopy:
+                    nc.vector.tensor_copy(out=dst, in_=src)
+                else:
+                    nc.scalar.copy(out=dst, in_=src)
+            return due
+
+        cb = const_psum.tile([P, 512], F32, name="cb", tag="cb")
 
         def build_tables():
-            cb = tp_pool.tile([P, 512], F32, name="cb", tag="tp")
             nc.tensor.matmul(out=cb[:, 0:272], lhsT=ones[:], rhs=vec_row[:], start=True, stop=True)
             for which in range(2):
                 w0 = which * HD
+                factor = math.log(S) if which == 0 else 1.0
                 tab = keep.tile([P, JT, 2, HD], F32, name="tab%d" % which, tag="tab%d" % which)
                 tables[which] = tab
-                nc.vector.tensor_tensor(
+                nc.vector.scalar_tensor_tensor(
                     out=tab[:, :, 0, :],
                     in0=cos_sb[:],
+                    scalar=factor,
                     in1=cb[:, w0 : w0 + HD].unsqueeze(1).to_broadcast([P, JT, HD]),
-                    op=MULT,
+                    op0=MULT,
+                    op1=MULT,
                 )
-                nc.vector.tensor_tensor(
+                nc.vector.scalar_tensor_tensor(
                     out=tab[:, :, 1, 0:HALF],
                     in0=sin_sb[:, :, HALF:HD],
+                    scalar=factor,
                     in1=cb[:, w0 : w0 + HALF].unsqueeze(1).to_broadcast([P, JT, HALF]),
-                    op=MULT,
+                    op0=MULT,
+                    op1=MULT,
                 )
                 nc.vector.scalar_tensor_tensor(
                     out=tab[:, :, 1, HALF:HD],
                     in0=sin_sb[:, :, 0:HALF],
-                    scalar=-1.0,
+                    scalar=-factor,
                     in1=cb[:, w0 + HALF : w0 + HD].unsqueeze(1).to_broadcast([P, JT, HALF]),
                     op0=MULT,
                     op1=MULT,
                 )
-            nc.vector.tensor_scalar(
-                out=gain[:, 0:NH], in0=cb[:, 2 * HD : 2 * HD + NH], scalar1=math.log(S), scalar2=None, op0=MULT
-            )
 
         def project(n, tt):
             acc = acc_pool.tile([P, 512], F32, name="acc", tag="acc")
@@ -218,22 +249,36 @@ def tile_biboattention_pa_kernel(
                 )
             return acc
 
-        def root_mean_square(acc):
+        def inverse_rms(acc):
             ss = stat_pool.tile([P, HPB], F32, name="ss", tag="ss")
             for h in range(HPB):
                 nc.scalar.activation(
                     out=junk[:], in_=acc[:, h * HD : (h + 1) * HD], func=ACT.Square, accum_out=ss[:, h : h + 1]
                 )
-            rms = stat_pool.tile([P, HPB], F32, name="rms", tag="rms")
-            nc.scalar.activation(out=rms[:], in_=ss[:], func=ACT.Sqrt, scale=1.0 / HD, bias=EPS)
-            return rms
+            root = stat_pool.tile([P, HPB], F32, name="root", tag="root")
+            if RSQRT:
+                nc.scalar.activation(out=root[:], in_=ss[:], func=ACT.Abs_reciprocal_sqrt, scale=1.0 / HD, bias=EPS)
+                return root
+            nc.scalar.activation(out=root[:], in_=ss[:], func=ACT.Sqrt, scale=1.0 / HD, bias=EPS)
+            rinv = stat_pool.tile([P, HPB], F32, name="rinv", tag="rinv")
+            nc.vector.reciprocal(out=rinv[:], in_=root[:])
+            return rinv
+
+        def head_factor(n, rinv):
+            if n >= NQ:
+                return rinv
+            rg = stat_pool.tile([P, HPB], F32, name="rg", tag="rg")
+            nc.vector.tensor_tensor(
+                out=rg[:], in0=rinv[:], in1=cb[:, 2 * HD + n * HPB : 2 * HD + (n + 1) * HPB], op=MULT
+            )
+            return rg
 
         def rope_head(blk, h):
             nc.vector.scalar_tensor_tensor(
                 out=blk["t12"][:, h, :, :],
-                in0=blk["acc"][:, h * HD : (h + 1) * HD].unsqueeze(1).to_broadcast([P, 2, HD]),
+                in0=tables[0 if blk["n"] < NQ else 1][:, blk["tt"] % JT, :, :],
                 scalar=blk["rg"][:, h : h + 1],
-                in1=tables[0 if blk["n"] < NQ else 1][:, blk["tt"] % JT, :, :],
+                in1=blk["acc"][:, h * HD : (h + 1) * HD].unsqueeze(1).to_broadcast([P, 2, HD]),
                 op0=MULT,
                 op1=MULT,
             )
@@ -247,59 +292,67 @@ def tile_biboattention_pa_kernel(
                 out_tiles[0] = out_pool.tile([P, HPB, JT, HD], F32, name="o_t", tag="o_t")
             o_t = out_tiles[0]
             t12 = blk["t12"]
-            nc.gpsimd.tensor_tensor(
+            eng = nc.gpsimd if ADD_ON_GPSIMD else nc.vector
+            eng.tensor_tensor(
                 out=o_t[:, :, j, 0:HALF], in0=t12[:, :, 0, 0:HALF], in1=t12[:, :, 1, HALF:HD], op=ADD
             )
-            nc.gpsimd.tensor_tensor(
+            eng.tensor_tensor(
                 out=o_t[:, :, j, HALF:HD], in0=t12[:, :, 0, HALF:HD], in1=t12[:, :, 1, 0:HALF], op=ADD
             )
-            if j == JT - 1:
-                if n < NQ:
-                    dst = out_0[b, n * HPB : (n + 1) * HPB]
-                else:
-                    dst = out_1[b]
+            if n < NQ:
+                dst = out_0[b, n * HPB : (n + 1) * HPB]
+            else:
+                dst = out_1[b]
+            if n == NT - 1 and b == B - 1:
+                nc.sync.dma_start(
+                    out=dst.rearrange("h (p j) d -> p h j d", j=JT)[:, :, j, :], in_=o_t[:, :, j, :]
+                )
+            elif j == JT - 1:
                 nc.sync.dma_start(
                     out=dst.rearrange("h (p j) d -> p h (j d)", j=JT),
                     in_=o_t[:].rearrange("p h j d -> p h (j d)"),
                 )
 
-        head = [("x", 0), ("x", 1), ("x", 2), ("x", 3), ("w", 0, 0), ("w", 0, 1), ("w", 0, 2), ("w", 0, 3)]
+        head = [("w", 0, 0), ("w", 0, 1), ("w", 0, 2), ("w", 0, 3), ("x", 0), ("x", 1)]
         for i, unit in enumerate(head):
-            done = prepare(unit)
-            quantize(done[0], done[1])
-            if i == 1:
+            for call in prepare(unit):
+                call()
+            if i == 0:
                 build_tables()
 
         after = units_after()
         waiting = []
         prev = None
+        older = None
         for m in range(NT * TT):
             n, tt = m // TT, m % TT
             blk = {"n": n, "tt": tt}
-            blk["acc"] = project(n, tt)
-            rms = root_mean_square(blk["acc"])
             if prev is not None:
                 prev["t12"] = rope_pool.tile([P, HPB, 2, HD], F32, name="t12", tag="t12")
                 rope_head(prev, 0)
                 rope_head(prev, 1)
-            for done in waiting:
-                quantize(done[0], done[1])
+            for call in waiting:
+                call()
             waiting = []
-            rinv = stat_pool.tile([P, HPB], F32, name="rinv", tag="rinv")
-            nc.vector.reciprocal(out=rinv[:], in_=rms[:])
+            blk["acc"] = project(n, tt)
+            rinv = inverse_rms(blk["acc"])
+            blk["rg"] = head_factor(n, rinv)
             if prev is not None:
                 rope_head(prev, 2)
-            blk["rg"] = stat_pool.tile([P, HPB], F32, name="rg", tag="rg")
-            nc.vector.tensor_tensor(
-                out=blk["rg"][:], in0=rinv[:], in1=gain[:, n * HPB : (n + 1) * HPB], op=MULT
-            )
-            if prev is not None:
                 rope_head(prev, 3)
-                finish(prev)
+                if ADD_ON_GPSIMD:
+                    finish(prev)
+            if older is not None and not ADD_ON_GPSIMD:
+                finish(older)
             for unit in after.get(m, []):
-                waiting.append(prepare(unit))
+                waiting.extend(prepare(unit))
+            older = prev
             prev = blk
         prev["t12"] = rope_pool.tile([P, HPB, 2, HD], F32, name="t12", tag="t12")
-        for h in range(HPB):
-            rope_head(prev, h)
+        rope_head(prev, 0)
+        rope_head(prev, 1)
+        if not ADD_ON_GPSIMD:
+            finish(older)
+        rope_head(prev, 2)
+        rope_head(prev, 3)
         finish(prev)

@@ -31,14 +31,15 @@ RSQRT = True
 
 def units_after():
     table = {}
-    table[0] = [("x", 2), ("x", 3)]
-    table[1] = [("w", 1, 0), ("w", 1, 1)]
-    table[2] = [("x", 4), ("x", 5)]
-    table[3] = [("w", 1, 2), ("w", 1, 3)]
-    table[4] = [("x", 6), ("x", 7)]
+    table[0] = [("x", 2), ("w", 1, 0)]
+    table[1] = [("x", 3), ("w", 1, 1)]
+    table[2] = [("x", 4), ("w", 1, 2)]
+    table[3] = [("x", 5), ("w", 1, 3)]
+    table[4] = [("x", 6)]
+    table[5] = [("x", 7)]
     for n in range(1, NT - 1):
-        table[n * TT + 1] = [("w", n + 1, 0), ("w", n + 1, 1)]
-        table[n * TT + 3] = [("w", n + 1, 2), ("w", n + 1, 3)]
+        for r in range(HPB):
+            table[n * TT + r] = [("w", n + 1, r)]
     return table
 
 
@@ -65,7 +66,9 @@ def tile_biboattention_pa_kernel(
         ident = keep.tile([P, P], F32, name="ident", tag="ident")
         make_identity(nc, ident[:])
         ones = keep.tile([P, P], BF16, name="ones", tag="ones")
-        nc.gpsimd.memset(ones[:], 1.0)
+        nc.vector.memset(ones[:], 1.0)
+        warm_rhs = keep.tile([P, 512], BF16, name="warm_rhs", tag="warm_rhs")
+        nc.vector.memset(warm_rhs[:], 0.0)
         warm = keep.tile([P, 1], F32, name="warm", tag="warm")
         nc.vector.memset(warm[:], 1.0)
         warm_out = keep.tile([P, 1], F32, name="warm_out", tag="warm_out")
@@ -104,14 +107,11 @@ def tile_biboattention_pa_kernel(
 
         for r in range(HPB):
             load_w(0, r)
-        for tt in range(4):
-            load_x(tt)
-        load_w(1, 0)
-        load_w(1, 1)
-        load_x(4)
-        load_x(5)
-        load_w(1, 2)
-        load_w(1, 3)
+        load_x(0)
+        load_x(1)
+        for r in range(HPB):
+            load_x(2 + r)
+            load_w(1, r)
         load_x(6)
         load_x(7)
         for r in range(HPB):
@@ -202,6 +202,11 @@ def tile_biboattention_pa_kernel(
             return due
 
         cb = const_psum.tile([P, 512], F32, name="cb", tag="cb")
+        warm_ps = acc_pool.tile([P, 512], F32, name="warm_ps", tag="acc")
+
+        def keep_warm(count):
+            for i in range(count):
+                nc.tensor.matmul(out=warm_ps[:], lhsT=ones[:], rhs=warm_rhs[:], start=True, stop=True)
 
         def build_tables():
             nc.tensor.matmul(out=cb[:, 0:272], lhsT=ones[:], rhs=vec_row[:], start=True, stop=True)
@@ -269,16 +274,16 @@ def tile_biboattention_pa_kernel(
                 return rinv
             rg = stat_pool.tile([P, HPB], F32, name="rg", tag="rg")
             nc.vector.tensor_tensor(
-                out=rg[:], in0=rinv[:], in1=cb[:, 2 * HD + n * HPB : 2 * HD + (n + 1) * HPB], op=MULT
+                out=rg[:], in0=cb[:, 2 * HD + n * HPB : 2 * HD + (n + 1) * HPB], in1=rinv[:], op=MULT
             )
             return rg
 
         def rope_head(blk, h):
             nc.vector.scalar_tensor_tensor(
                 out=blk["t12"][:, h, :, :],
-                in0=tables[0 if blk["n"] < NQ else 1][:, blk["tt"] % JT, :, :],
+                in0=blk["acc"][:, h * HD : (h + 1) * HD].unsqueeze(1).to_broadcast([P, 2, HD]),
                 scalar=blk["rg"][:, h : h + 1],
-                in1=blk["acc"][:, h * HD : (h + 1) * HD].unsqueeze(1).to_broadcast([P, 2, HD]),
+                in1=tables[0 if blk["n"] < NQ else 1][:, blk["tt"] % JT, :, :],
                 op0=MULT,
                 op1=MULT,
             )
@@ -314,9 +319,11 @@ def tile_biboattention_pa_kernel(
                 )
 
         head = [("w", 0, 0), ("w", 0, 1), ("w", 0, 2), ("w", 0, 3), ("x", 0), ("x", 1)]
+        keep_warm(8)
         for i, unit in enumerate(head):
             for call in prepare(unit):
                 call()
+            keep_warm(1)
             if i == 0:
                 build_tables()
 

@@ -25,7 +25,7 @@ HPB = 4
 NT = (NH + NKV) // HPB
 NQ = NH // HPB
 HALF = HD // 2
-ADD_ON_GPSIMD = True
+ADD_ON_GPSIMD = False
 RSQRT = True
 
 
@@ -56,9 +56,8 @@ def tile_biboattention_pa_kernel(
         stat_pool = ctx.enter_context(tc.tile_pool(name="stat", bufs=4))
         rope_pool = ctx.enter_context(tc.tile_pool(name="rope", bufs=3))
         out_pool = ctx.enter_context(tc.tile_pool(name="outp", bufs=3))
-        const_psum = ctx.enter_context(tc.psum_pool(name="constp", bufs=1))
         acc_pool = ctx.enter_context(tc.psum_pool(name="accp", bufs=4))
-        tp_pool = ctx.enter_context(tc.psum_pool(name="tpp", bufs=3))
+        tp_pool = ctx.enter_context(tc.psum_pool(name="tpp", bufs=4))
         ctx.enter_context(tc.manual_schedule())
 
         vec_row = keep.tile([P, 272], BF16, name="vec_row", tag="vec_row")
@@ -201,7 +200,7 @@ def tile_biboattention_pa_kernel(
                     nc.scalar.copy(out=dst, in_=src)
             return due
 
-        cb = const_psum.tile([P, 512], F32, name="cb", tag="cb")
+        gain = keep.tile([P, NH], F32, name="gain", tag="gain")
         warm_ps = acc_pool.tile([P, 512], F32, name="warm_ps", tag="acc")
 
         def keep_warm(count):
@@ -209,6 +208,7 @@ def tile_biboattention_pa_kernel(
                 nc.tensor.matmul(out=warm_ps[:], lhsT=ones[:], rhs=warm_rhs[:], start=True, stop=True)
 
         def build_tables():
+            cb = tp_pool.tile([P, 512], F32, name="cb", tag="tp")
             nc.tensor.matmul(out=cb[:, 0:272], lhsT=ones[:], rhs=vec_row[:], start=True, stop=True)
             for which in range(2):
                 w0 = which * HD
@@ -239,6 +239,7 @@ def tile_biboattention_pa_kernel(
                     op0=MULT,
                     op1=MULT,
                 )
+            nc.vector.tensor_copy(out=gain[:], in_=cb[:, 2 * HD : 2 * HD + NH])
 
         def project(n, tt):
             acc = acc_pool.tile([P, 512], F32, name="acc", tag="acc")
@@ -273,9 +274,7 @@ def tile_biboattention_pa_kernel(
             if n >= NQ:
                 return rinv
             rg = stat_pool.tile([P, HPB], F32, name="rg", tag="rg")
-            nc.vector.tensor_tensor(
-                out=rg[:], in0=cb[:, 2 * HD + n * HPB : 2 * HD + (n + 1) * HPB], in1=rinv[:], op=MULT
-            )
+            nc.gpsimd.tensor_tensor(out=rg[:], in0=rinv[:], in1=gain[:, n * HPB : (n + 1) * HPB], op=MULT)
             return rg
 
         def rope_head(blk, h):
@@ -299,10 +298,10 @@ def tile_biboattention_pa_kernel(
             t12 = blk["t12"]
             eng = nc.gpsimd if ADD_ON_GPSIMD else nc.vector
             eng.tensor_tensor(
-                out=o_t[:, :, j, 0:HALF], in0=t12[:, :, 0, 0:HALF], in1=t12[:, :, 1, HALF:HD], op=ADD
-            )
-            eng.tensor_tensor(
-                out=o_t[:, :, j, HALF:HD], in0=t12[:, :, 0, HALF:HD], in1=t12[:, :, 1, 0:HALF], op=ADD
+                out=o_t[:, :, j, :].rearrange("p h (u i) -> p h u i", u=2),
+                in0=t12[:, :, 0, :].rearrange("p h (u i) -> p h u i", u=2),
+                in1=t12[:, :, 1, :].rearrange("p h (u i) -> p h u i", u=2)[:, :, ::-1, :],
+                op=ADD,
             )
             if n < NQ:
                 dst = out_0[b, n * HPB : (n + 1) * HPB]

@@ -25,7 +25,7 @@ HPB = 4
 NT = (NH + NKV) // HPB
 NQ = NH // HPB
 HALF = HD // 2
-ADD_ON_GPSIMD = False
+ADD_ON_GPSIMD = True
 RSQRT = True
 
 
@@ -38,8 +38,8 @@ def units_after():
     table[4] = [("x", 6)]
     table[5] = [("x", 7)]
     for n in range(1, NT - 1):
-        for r in range(HPB):
-            table[n * TT + r] = [("w", n + 1, r)]
+        for r, place in enumerate((0, 1, 3, 4)):
+            table[n * TT + place] = [("w", n + 1, r)]
     return table
 
 
@@ -71,7 +71,6 @@ def tile_biboattention_pa_kernel(
         warm = keep.tile([P, 1], F32, name="warm", tag="warm")
         nc.vector.memset(warm[:], 1.0)
         warm_out = keep.tile([P, 1], F32, name="warm_out", tag="warm_out")
-        junk = keep.tile([P, HD], F32, name="junk", tag="junk")
 
         cos_sb = keep.tile([P, JT, HD], BF16, name="cos_sb", tag="cos_sb")
         sin_sb = keep.tile([P, JT, HD], BF16, name="sin_sb", tag="sin_sb")
@@ -122,7 +121,7 @@ def tile_biboattention_pa_kernel(
         w_scales = {}
         w_grouped = {}
         tables = {}
-        vcopy = []
+        vcopy = [("w", 1)]
 
         def transposes(words):
             banks = []
@@ -257,9 +256,13 @@ def tile_biboattention_pa_kernel(
 
         def inverse_rms(acc):
             ss = stat_pool.tile([P, HPB], F32, name="ss", tag="ss")
+            squares = rope_pool.tile([P, HPB, HD], F32, name="squares", tag="squares")
             for h in range(HPB):
                 nc.scalar.activation(
-                    out=junk[:], in_=acc[:, h * HD : (h + 1) * HD], func=ACT.Square, accum_out=ss[:, h : h + 1]
+                    out=squares[:, h, :],
+                    in_=acc[:, h * HD : (h + 1) * HD],
+                    func=ACT.Square,
+                    accum_out=ss[:, h : h + 1],
                 )
             root = stat_pool.tile([P, HPB], F32, name="root", tag="root")
             if RSQRT:
@@ -298,10 +301,10 @@ def tile_biboattention_pa_kernel(
             t12 = blk["t12"]
             eng = nc.gpsimd if ADD_ON_GPSIMD else nc.vector
             eng.tensor_tensor(
-                out=o_t[:, :, j, :].rearrange("p h (u i) -> p h u i", u=2),
-                in0=t12[:, :, 0, :].rearrange("p h (u i) -> p h u i", u=2),
-                in1=t12[:, :, 1, :].rearrange("p h (u i) -> p h u i", u=2)[:, :, ::-1, :],
-                op=ADD,
+                out=o_t[:, :, j, 0:HALF], in0=t12[:, :, 0, 0:HALF], in1=t12[:, :, 1, HALF:HD], op=ADD
+            )
+            eng.tensor_tensor(
+                out=o_t[:, :, j, HALF:HD], in0=t12[:, :, 0, HALF:HD], in1=t12[:, :, 1, 0:HALF], op=ADD
             )
             if n < NQ:
                 dst = out_0[b, n * HPB : (n + 1) * HPB]

@@ -300,11 +300,12 @@ def tile_biboattention_pa_kernel(
             o_t = out_tiles[0]
             t12 = blk["t12"]
             eng = nc.gpsimd if ADD_ON_GPSIMD else nc.vector
+            halves = t12[:].rearrange("p h t (u i) -> p h t u i", u=2)
             eng.tensor_tensor(
-                out=o_t[:, :, j, 0:HALF], in0=t12[:, :, 0, 0:HALF], in1=t12[:, :, 1, HALF:HD], op=ADD
-            )
-            eng.tensor_tensor(
-                out=o_t[:, :, j, HALF:HD], in0=t12[:, :, 0, HALF:HD], in1=t12[:, :, 1, 0:HALF], op=ADD
+                out=o_t[:, :, j, :].rearrange("p h (u i) -> p h u i", u=2),
+                in0=halves[:, :, 0, :, :],
+                in1=halves[:, :, 1, ::-1, :],
+                op=ADD,
             )
             if n < NQ:
                 dst = out_0[b, n * HPB : (n + 1) * HPB]

@@ -121,7 +121,7 @@ def tile_biboattention_pa_kernel(
         w_scales = {}
         w_grouped = {}
         tables = {}
-        vcopy = [("w", 1)]
+        vcopy = []
 
         def transposes(words):
             banks = []

@@ -341,9 +341,6 @@ def tile_biboattention_pa_kernel(
                 prev["t12"] = rope_pool.tile([P, HPB, 2, HD], F32, name="t12", tag="t12")
                 rope_head(prev, 0)
                 rope_head(prev, 1)
-            for call in waiting:
-                call()
-            waiting = []
             blk["acc"] = project(n, tt)
             rinv = inverse_rms(blk["acc"])
             blk["rg"] = head_factor(n, rinv)
@@ -354,6 +351,9 @@ def tile_biboattention_pa_kernel(
                     finish(prev)
             if older is not None and not ADD_ON_GPSIMD:
                 finish(older)
+            for call in waiting:
+                call()
+            waiting = []
             for unit in after.get(m, []):
                 waiting.extend(prepare(unit))
             older = prev

@@ -31,12 +31,11 @@ RSQRT = True
 
 def units_after():
     table = {}
-    table[0] = [("x", 2), ("w", 1, 0)]
-    table[1] = [("x", 3), ("w", 1, 1)]
-    table[2] = [("x", 4), ("w", 1, 2)]
-    table[3] = [("x", 5), ("w", 1, 3)]
-    table[4] = [("x", 6)]
-    table[5] = [("x", 7)]
+    table[0] = [("x", 2), ("x", 3)]
+    table[1] = [("x", 4), ("w", 1, 0)]
+    table[2] = [("x", 5), ("w", 1, 1)]
+    table[3] = [("x", 6), ("w", 1, 2)]
+    table[4] = [("x", 7), ("w", 1, 3)]
     for n in range(1, NT - 1):
         for r, place in enumerate((0, 1, 3, 4)):
             table[n * TT + place] = [("w", n + 1, r)]
@@ -107,11 +106,11 @@ def tile_biboattention_pa_kernel(
             load_w(0, r)
         load_x(0)
         load_x(1)
+        load_x(2)
+        load_x(3)
         for r in range(HPB):
-            load_x(2 + r)
+            load_x(4 + r)
             load_w(1, r)
-        load_x(6)
-        load_x(7)
         for r in range(HPB):
             load_w(2, r)
 

@@ -120,7 +120,7 @@ def tile_biboattention_pa_kernel(
         w_scales = {}
         w_grouped = {}
         tables = {}
-        vcopy = []
+        vcopy = [("x", 1)]
 
         def transposes(words):
             banks = []

@@ -102,9 +102,9 @@ def tile_biboattention_pa_kernel(
                 rows = wk[r * P : (r + 1) * P, :]
             nc.sync.dma_start(out=w_raw[n][:, r, :], in_=rows)
 
+        load_x(0)
         for r in range(HPB):
             load_w(0, r)
-        load_x(0)
         load_x(1)
         load_x(2)
         load_x(3)
@@ -205,10 +205,10 @@ def tile_biboattention_pa_kernel(
             for i in range(count):
                 nc.tensor.matmul(out=warm_ps[:], lhsT=ones[:], rhs=warm_rhs[:], start=True, stop=True)
 
-        def build_tables():
+        def build_tables(first, last):
             cb = tp_pool.tile([P, 512], F32, name="cb", tag="tp")
             nc.tensor.matmul(out=cb[:, 0:272], lhsT=ones[:], rhs=vec_row[:], start=True, stop=True)
-            for which in range(2):
+            for which in range(first, last):
                 w0 = which * HD
                 factor = math.log(S) if which == 0 else 1.0
                 tab = keep.tile([P, JT, 2, HD], F32, name="tab%d" % which, tag="tab%d" % which)
@@ -237,7 +237,8 @@ def tile_biboattention_pa_kernel(
                     op0=MULT,
                     op1=MULT,
                 )
-            nc.vector.tensor_copy(out=gain[:], in_=cb[:, 2 * HD : 2 * HD + NH])
+            if first == 0:
+                nc.vector.tensor_copy(out=gain[:], in_=cb[:, 2 * HD : 2 * HD + NH])
 
         def project(n, tt):
             acc = acc_pool.tile([P, 512], F32, name="acc", tag="acc")
@@ -298,7 +299,7 @@ def tile_biboattention_pa_kernel(
                 out_tiles[0] = out_pool.tile([P, HPB, JT, HD], F32, name="o_t", tag="o_t")
             o_t = out_tiles[0]
             t12 = blk["t12"]
-            eng = nc.gpsimd if ADD_ON_GPSIMD else nc.vector
+            eng = nc.vector if (n == NT - 1 and tt == TT - 1) else nc.gpsimd
             halves = t12[:].rearrange("p h t (u i) -> p h t u i", u=2)
             eng.tensor_tensor(
                 out=o_t[:, :, j, :].rearrange("p h (u i) -> p h u i", u=2),
@@ -320,14 +321,14 @@ def tile_biboattention_pa_kernel(
                     in_=o_t[:].rearrange("p h j d -> p h (j d)"),
                 )
 
-        head = [("w", 0, 0), ("w", 0, 1), ("w", 0, 2), ("w", 0, 3), ("x", 0), ("x", 1)]
-        keep_warm(8)
+        head = [("x", 0), ("w", 0, 0), ("w", 0, 1), ("w", 0, 2), ("w", 0, 3), ("x", 1)]
+        keep_warm(3)
         for i, unit in enumerate(head):
             for call in prepare(unit):
                 call()
             keep_warm(1)
             if i == 0:
-                build_tables()
+                build_tables(0, 1)
 
         after = units_after()
         waiting = []
@@ -353,6 +354,8 @@ def tile_biboattention_pa_kernel(
             for call in waiting:
                 call()
             waiting = []
+            if m == TT - 2:
+                build_tables(1, 2)
             for unit in after.get(m, []):
                 waiting.extend(prepare(unit))
             older = prev

@@ -108,9 +108,14 @@ def tile_biboattention_pa_kernel(
         load_x(1)
         load_x(2)
         load_x(3)
-        for r in range(HPB):
-            load_x(4 + r)
-            load_w(1, r)
+        load_x(4)
+        load_w(1, 0)
+        load_w(1, 1)
+        load_x(5)
+        load_w(1, 2)
+        load_w(1, 3)
+        load_x(6)
+        load_x(7)
         for r in range(HPB):
             load_w(2, r)
 
@@ -122,19 +127,16 @@ def tile_biboattention_pa_kernel(
         tables = {}
         vcopy = [("x", 1)]
 
-        def transposes(words):
-            banks = []
-            for half in range(2):
-                tp = tp_pool.tile([P, 512], F32, name="tp", tag="tp")
-                for gg in range(2):
-                    g = 2 * half + gg
-                    for u in range(2):
-                        c = 2 * gg + u
-                        nc.tensor.transpose(
-                            tp[:, c * P : (c + 1) * P], words[:, 256 * g + u : 256 * (g + 1) : 2], ident[:]
-                        )
-                banks.append(tp)
-            return banks
+        def transposes(words, half):
+            tp = tp_pool.tile([P, 512], F32, name="tp", tag="tp")
+            for gg in range(2):
+                g = 2 * half + gg
+                for u in range(2):
+                    c = 2 * gg + u
+                    nc.tensor.transpose(
+                        tp[:, c * P : (c + 1) * P], words[:, 256 * g + u : 256 * (g + 1) : 2], ident[:]
+                    )
+            return tp
 
         def quantize_x(tt, grouped):
             nc.vector.quantize_mx(
@@ -164,6 +166,7 @@ def tile_biboattention_pa_kernel(
                 words = x_raw[tt // JT][:, tt % JT, :].bitcast(F32)
                 grouped = grpx_pool.tile([P, PASSES, P, 4], BF16, name="x_grouped", tag="x_grouped", align_bytes=64)
                 gwords = grouped[:].bitcast(F32)
+                parts = [(words, half, gwords[:, 2 * half : 2 * half + 2, :, :]) for half in range(2)]
                 due = [lambda: quantize_x(tt, grouped)]
             else:
                 n, r = unit[1], unit[2]
@@ -177,22 +180,25 @@ def tile_biboattention_pa_kernel(
                     w_grouped[n] = grpw_pool.tile(
                         [P, PASSES, HPB, P, 4], BF16, name="w_grouped", tag="w_grouped", align_bytes=64
                     )
-                words = w_raw[n][:, r, :].bitcast(F32)
-                gwords = w_grouped[n][:].bitcast(F32)[:, :, r, :, :]
+                gwords = w_grouped[n][:].bitcast(F32)
                 if n == 0:
+                    pairs = [(r, 0), (r, 1)]
                     due = [lambda: quantize_w_tile(n, r)]
-                elif r == HPB - 1:
-                    due = [lambda: quantize_w_passes(n, 0), lambda: quantize_w_passes(n, 1)]
                 else:
-                    due = []
-            banks = transposes(words)
+                    pairs = [(2 * (r % 2), r // 2), (2 * (r % 2) + 1, r // 2)]
+                    due = [lambda: quantize_w_passes(n, r // 2)] if r % 2 == 1 else []
+                parts = [
+                    (w_raw[n][:, row, :].bitcast(F32), half, gwords[:, 2 * half : 2 * half + 2, row, :, :])
+                    for row, half in pairs
+                ]
+            banks = [transposes(words, half) for words, half, dst in parts]
             if unit[0] == "w" and unit[2] == HPB - 1 and unit[1] + 3 < NT:
                 for row in range(HPB):
                     load_w(unit[1] + 3, row)
-            for half in range(2):
-                dst = gwords[:, 2 * half : 2 * half + 2, :, :]
-                src = banks[half][:].rearrange("p (g u r) -> p g r u", g=2, u=2)
-                if (unit[0], half) in vcopy:
+            for i in range(2):
+                dst = parts[i][2]
+                src = banks[i][:].rearrange("p (g u r) -> p g r u", g=2, u=2)
+                if (unit[0], i) in vcopy:
                     nc.vector.tensor_copy(out=dst, in_=src)
                 else:
                     nc.scalar.copy(out=dst, in_=src)

@@ -262,7 +262,7 @@ def tile_biboattention_pa_kernel(
 
         def inverse_rms(acc):
             ss = stat_pool.tile([P, HPB], F32, name="ss", tag="ss")
-            squares = rope_pool.tile([P, HPB, HD], F32, name="squares", tag="squares")
+            squares = rope_pool.tile([P, HPB, HD], BF16, name="squares", tag="squares")
             for h in range(HPB):
                 nc.scalar.activation(
                     out=squares[:, h, :],

@@ -31,15 +31,19 @@ RSQRT = True
 
 def units_after():
     table = {}
-    table[0] = [("x", 2), ("x", 3)]
-    table[1] = [("x", 4), ("w", 1, 0)]
-    table[2] = [("x", 5), ("w", 1, 1)]
-    table[3] = [("x", 6), ("w", 1, 2)]
-    table[4] = [("x", 7), ("w", 1, 3)]
+    table[0] = [("x", 2)]
+    table[1] = [("x", 4)]
+    table[2] = [("x", 5)]
+    table[3] = [("x", 6)]
+    table[4] = [("x", 7)]
     for n in range(1, NT - 1):
         for r, place in enumerate((0, 1, 3, 4)):
             table[n * TT + place] = [("w", n + 1, r)]
     return table
+
+
+def units_between():
+    return {1: [("x", 3)], 2: [("w", 1, 0)], 3: [("w", 1, 1)], 4: [("w", 1, 2)], 5: [("w", 1, 3)]}
 
 
 def tile_biboattention_pa_kernel(
@@ -160,7 +164,7 @@ def tile_biboattention_pa_kernel(
                 in_=w_grouped[n][:, 2 * c : 2 * c + 2, :, :, :].rearrange("p g h r t -> p (g h r t)"),
             )
 
-        def prepare(unit):
+        def prepare(unit, scalar_only=False):
             if unit[0] == "x":
                 tt = unit[1]
                 words = x_raw[tt // JT][:, tt % JT, :].bitcast(F32)
@@ -198,7 +202,7 @@ def tile_biboattention_pa_kernel(
             for i in range(2):
                 dst = parts[i][2]
                 src = banks[i][:].rearrange("p (g u r) -> p g r u", g=2, u=2)
-                if (unit[0], i) in vcopy:
+                if (unit[0], i) in vcopy and not scalar_only:
                     nc.vector.tensor_copy(out=dst, in_=src)
                 else:
                     nc.scalar.copy(out=dst, in_=src)
@@ -246,9 +250,8 @@ def tile_biboattention_pa_kernel(
             if first == 0:
                 nc.vector.tensor_copy(out=gain[:], in_=cb[:, 2 * HD : 2 * HD + NH])
 
-        def project(n, tt):
-            acc = acc_pool.tile([P, 512], F32, name="acc", tag="acc")
-            for g in range(PASSES):
+        def project(acc, n, tt, first, last):
+            for g in range(first, last):
                 nc.tensor.matmul_mx(
                     out=acc[:],
                     lhsT=x_codes[:, tt, g, :].bitcast(E5X4),
@@ -258,7 +261,6 @@ def tile_biboattention_pa_kernel(
                     start=(g == 0),
                     stop=(g == PASSES - 1),
                 )
-            return acc
 
         def inverse_rms(acc):
             ss = stat_pool.tile([P, HPB], F32, name="ss", tag="ss")
@@ -337,6 +339,7 @@ def tile_biboattention_pa_kernel(
                 build_tables(0, 1)
 
         after = units_after()
+        between = units_between()
         waiting = []
         prev = None
         older = None
@@ -347,7 +350,11 @@ def tile_biboattention_pa_kernel(
                 prev["t12"] = rope_pool.tile([P, HPB, 2, HD], F32, name="t12", tag="t12")
                 rope_head(prev, 0)
                 rope_head(prev, 1)
-            blk["acc"] = project(n, tt)
+            blk["acc"] = acc_pool.tile([P, 512], F32, name="acc", tag="acc")
+            project(blk["acc"], n, tt, 0, PASSES // 2)
+            for unit in between.get(m, []):
+                waiting.extend(prepare(unit, scalar_only=True))
+            project(blk["acc"], n, tt, PASSES // 2, PASSES)
             rinv = inverse_rms(blk["acc"])
             blk["rg"] = head_factor(n, rinv)
             if prev is not None:

@@ -60,7 +60,8 @@ def tile_biboattention_pa_kernel(
         rope_pool = ctx.enter_context(tc.tile_pool(name="rope", bufs=3))
         out_pool = ctx.enter_context(tc.tile_pool(name="outp", bufs=3))
         acc_pool = ctx.enter_context(tc.psum_pool(name="accp", bufs=4))
-        tp_pool = ctx.enter_context(tc.psum_pool(name="tpp", bufs=4))
+        tp_pool = ctx.enter_context(tc.psum_pool(name="tpp", bufs=3))
+        flex_pool = ctx.enter_context(tc.psum_pool(name="flexp", bufs=1))
         ctx.enter_context(tc.manual_schedule())
 
         vec_row = keep.tile([P, 272], BF16, name="vec_row", tag="vec_row")
@@ -131,8 +132,29 @@ def tile_biboattention_pa_kernel(
         tables = {}
         vcopy = [("x", 1)]
 
+        counts = {"tp": 0, "acc": 0, "late": 0}
+
+        def transpose_bank():
+            k = counts["tp"]
+            counts["tp"] = k + 1
+            if counts["late"] == 0 and k % 4 == 3:
+                bank = flex_pool.tile([P, 512], F32, name="tp_flex", tag="flex")
+            else:
+                bank = tp_pool.tile([P, 512], F32, name="tp", tag="tp")
+            return bank
+
+        def result_bank():
+            k = counts["acc"]
+            if counts["late"] == 1:
+                counts["acc"] = k + 1
+            if counts["late"] == 1 and k % 5 == 4:
+                bank = flex_pool.tile([P, 512], F32, name="acc_flex", tag="flex")
+            else:
+                bank = acc_pool.tile([P, 512], F32, name="acc", tag="acc")
+            return bank
+
         def transposes(words, half):
-            tp = tp_pool.tile([P, 512], F32, name="tp", tag="tp")
+            tp = transpose_bank()
             for gg in range(2):
                 g = 2 * half + gg
                 for u in range(2):
@@ -350,7 +372,9 @@ def tile_biboattention_pa_kernel(
                 prev["t12"] = rope_pool.tile([P, HPB, 2, HD], F32, name="t12", tag="t12")
                 rope_head(prev, 0)
                 rope_head(prev, 1)
-            blk["acc"] = acc_pool.tile([P, 512], F32, name="acc", tag="acc")
+            if m == TT - 2:
+                counts["late"] = 1
+            blk["acc"] = result_bank()
             project(blk["acc"], n, tt, 0, PASSES // 2)
             for unit in between.get(m, []):
                 waiting.extend(prepare(unit, scalar_only=True))

@@ -147,10 +147,7 @@ def tile_biboattention_pa_kernel(
             k = counts["acc"]
             if counts["late"] == 1:
                 counts["acc"] = k + 1
-            if counts["late"] == 1 and k % 5 == 4:
-                bank = flex_pool.tile([P, 512], F32, name="acc_flex", tag="flex")
-            else:
-                bank = acc_pool.tile([P, 512], F32, name="acc", tag="acc")
+            bank = acc_pool.tile([P, 512], F32, name="acc", tag="acc")
             return bank
 
         def transposes(words, half):
@@ -231,6 +228,7 @@ def tile_biboattention_pa_kernel(
             return due
 
         gain = keep.tile([P, NH], F32, name="gain", tag="gain")
+        kept = {}
         warm_ps = acc_pool.tile([P, 512], F32, name="warm_ps", tag="acc")
 
         def keep_warm(count):
@@ -238,7 +236,11 @@ def tile_biboattention_pa_kernel(
                 nc.tensor.matmul(out=warm_ps[:], lhsT=ones[:], rhs=warm_rhs[:], start=True, stop=True)
 
         def build_tables(first, last):
-            cb = tp_pool.tile([P, 512], F32, name="cb", tag="tp")
+            if first == 0:
+                cb = tp_pool.tile([P, 512], F32, name="cb", tag="tp")
+            else:
+                cb = flex_pool.tile([P, 512], F32, name="cb_kept", tag="flex")
+                kept["cb"] = cb
             nc.tensor.matmul(out=cb[:, 0:272], lhsT=ones[:], rhs=vec_row[:], start=True, stop=True)
             for which in range(first, last):
                 w0 = which * HD
@@ -307,7 +309,12 @@ def tile_biboattention_pa_kernel(
             if n >= NQ:
                 return rinv
             rg = stat_pool.tile([P, HPB], F32, name="rg", tag="rg")
-            nc.gpsimd.tensor_tensor(out=rg[:], in0=rinv[:], in1=gain[:, n * HPB : (n + 1) * HPB], op=MULT)
+            if n == 0:
+                nc.gpsimd.tensor_tensor(out=rg[:], in0=rinv[:], in1=gain[:, n * HPB : (n + 1) * HPB], op=MULT)
+            else:
+                nc.vector.tensor_tensor(
+                    out=rg[:], in0=rinv[:], in1=kept["cb"][:, 2 * HD + n * HPB : 2 * HD + (n + 1) * HPB], op=MULT
+                )
             return rg
 
         def rope_head(blk, h):

@@ -221,7 +221,7 @@ def tile_biboattention_pa_kernel(
             for i in range(2):
                 dst = parts[i][2]
                 src = banks[i][:].rearrange("p (g u r) -> p g r u", g=2, u=2)
-                if (unit[0], i) in vcopy and not scalar_only:
+                if ((unit[0], i) in vcopy or (unit[0] == "w" and unit[1] >= 2 and unit[2] % 2 == 1 and i == 1)) and not scalar_only:
                     nc.vector.tensor_copy(out=dst, in_=src)
                 else:
                     nc.scalar.copy(out=dst, in_=src)

import math
from contextlib import ExitStack

import concourse.mybir as mybir
from concourse.masks import make_identity

B, S, H, NH, NKV, HD = 2, 512, 2048, 16, 4, 128
EPS = 1e-6
FLOPS = 2 * B * S * H * (NH + NKV) * HD

F32 = mybir.dt.float32
BF16 = mybir.dt.bfloat16
U32 = mybir.dt.uint32
U8 = mybir.dt.uint8
E5X4 = mybir.dt.float8_e5m2_x4
MULT = mybir.AluOpType.mult
ADD = mybir.AluOpType.add
ACT = mybir.ActivationFunctionType

P = 128
PASSES = H // 512
JT = S // P
TT = B * JT
HPB = 4
NT = (NH + NKV) // HPB
NQ = NH // HPB
HALF = HD // 2
ADD_ON_GPSIMD = True
RSQRT = True


def units_after():
    table = {}
    table[0] = [("x", 2)]
    table[1] = [("x", 4)]
    table[2] = [("x", 5)]
    table[3] = [("x", 6)]
    table[4] = [("x", 7)]
    for n in range(1, NT - 1):
        for r, place in enumerate((0, 1, 3, 4)):
            table[n * TT + place] = [("w", n + 1, r)]
    return table


def units_between():
    return {1: [("x", 3)], 2: [("w", 1, 0)], 3: [("w", 1, 1)], 4: [("w", 1, 2)], 5: [("w", 1, 3)]}


def tile_biboattention_pa_kernel(
    tc, hidden_states, cos, sin, wq, wk, q_norm_w, k_norm_w, ssmax_scale, out_0, out_1
):
    nc = tc.nc
    with ExitStack() as ctx:
        keep = ctx.enter_context(tc.tile_pool(name="keep", bufs=1))
        wraw_pool = ctx.enter_context(tc.tile_pool(name="wraw", bufs=3))
        wcode_pool = ctx.enter_context(tc.tile_pool(name="wcode", bufs=2))
        grpw_pool = ctx.enter_context(tc.tile_pool(name="grpw", bufs=2))
        grpx_pool = ctx.enter_context(tc.tile_pool(name="grpx", bufs=3))
        stat_pool = ctx.enter_context(tc.tile_pool(name="stat", bufs=4))
        rope_pool = ctx.enter_context(tc.tile_pool(name="rope", bufs=3))
        out_pool = ctx.enter_context(tc.tile_pool(name="outp", bufs=3))
        acc_pool = ctx.enter_context(tc.psum_pool(name="accp", bufs=4))
        tp_pool = ctx.enter_context(tc.psum_pool(name="tpp", bufs=3))
        flex_pool = ctx.enter_context(tc.psum_pool(name="flexp", bufs=1))
        ctx.enter_context(tc.manual_schedule())

        vec_row = keep.tile([P, 272], BF16, name="vec_row", tag="vec_row")
        nc.gpsimd.memset(vec_row[:], 0.0)
        ident = keep.tile([P, P], F32, name="ident", tag="ident")
        make_identity(nc, ident[:])
        ones = keep.tile([P, P], BF16, name="ones", tag="ones")
        nc.vector.memset(ones[:], 1.0)
        warm_rhs = keep.tile([P, 512], BF16, name="warm_rhs", tag="warm_rhs")
        nc.vector.memset(warm_rhs[:], 0.0)
        warm = keep.tile([P, 1], F32, name="warm", tag="warm")
        nc.vector.memset(warm[:], 1.0)
        warm_out = keep.tile([P, 1], F32, name="warm_out", tag="warm_out")

        cos_sb = keep.tile([P, JT, HD], BF16, name="cos_sb", tag="cos_sb")
        sin_sb = keep.tile([P, JT, HD], BF16, name="sin_sb", tag="sin_sb")
        nc.scalar.dma_start(out=vec_row[0:1, 0:HD], in_=q_norm_w.rearrange("(o d) -> o d", o=1))
        nc.scalar.dma_start(out=vec_row[0:1, HD : 2 * HD], in_=k_norm_w.rearrange("(o d) -> o d", o=1))
        nc.scalar.dma_start(
            out=vec_row[0:1, 2 * HD : 2 * HD + NH], in_=ssmax_scale.rearrange("a h b c -> a (h b c)")
        )
        nc.scalar.dma_start(out=cos_sb[:], in_=cos.rearrange("(p j) d -> p j d", j=JT))
        nc.scalar.dma_start(out=sin_sb[:], in_=sin.rearrange("(p j) d -> p j d", j=JT))
        nc.scalar.activation(
            out=warm_out[:], in_=warm[:], func=(ACT.Abs_reciprocal_sqrt if RSQRT else ACT.Sqrt)
        )

        x_raw = []
        for b in range(B):
            x_raw.append(keep.tile([P, JT, H], BF16, name="x_raw%d" % b, tag="x_raw%d" % b))
        w_raw = {}

        def load_x(tt):
            src = hidden_states[tt // JT].rearrange("(p j) k -> p j k", j=JT)
            nc.sync.dma_start(out=x_raw[tt // JT][:, tt % JT, :], in_=src[:, tt % JT, :])

        def load_w(n, r):
            if r == 0:
                w_raw[n] = wraw_pool.tile([P, HPB, H], BF16, name="w_raw", tag="w_raw")
            if n < NQ:
                rows = wq[(n * HPB + r) * P : (n * HPB + r + 1) * P, :]
            else:
                rows = wk[r * P : (r + 1) * P, :]
            nc.sync.dma_start(out=w_raw[n][:, r, :], in_=rows)

        load_x(0)
        for r in range(HPB):
            load_w(0, r)
        load_x(1)
        load_x(2)
        load_x(3)
        load_x(4)
        load_w(1, 0)
        load_w(1, 1)
        load_x(5)
        load_w(1, 2)
        load_w(1, 3)
        load_x(6)
        load_x(7)
        for r in range(HPB):
            load_w(2, r)

        x_codes = keep.tile([P, TT, PASSES, P], U32, name="x_codes", tag="x_codes", align_bytes=64)
        x_scales = keep.tile([P, TT, PASSES, P], U8, name="x_scales", tag="x_scales", align_bytes=64)
        w_codes = {}
        w_scales = {}
        w_grouped = {}
        tables = {}
        vcopy = [("x", 1)]

        counts = {"tp": 0, "acc": 0, "late": 0}

        def transpose_bank():
            k = counts["tp"]
            counts["tp"] = k + 1
            if counts["late"] == 0 and k % 4 == 3:
                bank = flex_pool.tile([P, 512], F32, name="tp_flex", tag="flex")
            else:
                bank = tp_pool.tile([P, 512], F32, name="tp", tag="tp")
            return bank

        def result_bank():
            k = counts["acc"]
            if counts["late"] == 1:
                counts["acc"] = k + 1
            bank = acc_pool.tile([P, 512], F32, name="acc", tag="acc")
            return bank

        def transposes(words, half):
            tp = transpose_bank()
            for gg in range(2):
                g = 2 * half + gg
                for u in range(2):
                    c = 2 * gg + u
                    nc.tensor.transpose(
                        tp[:, c * P : (c + 1) * P], words[:, 256 * g + u : 256 * (g + 1) : 2], ident[:]
                    )
            return tp

        def quantize_x(tt, grouped):
            nc.vector.quantize_mx(
                out=x_codes[:, tt, :, :].rearrange("p g r -> p (g r)").bitcast(E5X4),
                scales=x_scales[:, tt, :, :].rearrange("p g r -> p (g r)"),
                in_=grouped[:].rearrange("p g r t -> p (g r t)"),
            )

        def quantize_w_tile(n, r):
            for g in range(PASSES):
                nc.vector.quantize_mx(
                    out=w_codes[n][:, g, r * P : (r + 1) * P].bitcast(E5X4),
                    scales=w_scales[n][:, g, r * P : (r + 1) * P],
                    in_=w_grouped[n][:, g, r, :, :].rearrange("p r t -> p (r t)"),
                )

        def quantize_w_passes(n, c):
            nc.vector.quantize_mx(
                out=w_codes[n][:, 2 * c : 2 * c + 2, :].rearrange("p g c -> p (g c)").bitcast(E5X4),
                scales=w_scales[n][:, 2 * c : 2 * c + 2, :].rearrange("p g c -> p (g c)"),
                in_=w_grouped[n][:, 2 * c : 2 * c + 2, :, :, :].rearrange("p g h r t -> p (g h r t)"),
            )

        def prepare(unit, scalar_only=False):
            if unit[0] == "x":
                tt = unit[1]
                words = x_raw[tt // JT][:, tt % JT, :].bitcast(F32)
                grouped = grpx_pool.tile([P, PASSES, P, 4], BF16, name="x_grouped", tag="x_grouped", align_bytes=64)
                gwords = grouped[:].bitcast(F32)
                parts = [(words, half, gwords[:, 2 * half : 2 * half + 2, :, :]) for half in range(2)]
                due = [lambda: quantize_x(tt, grouped)]
            else:
                n, r = unit[1], unit[2]
                if r == 0:
                    w_codes[n] = wcode_pool.tile(
                        [P, PASSES, 512], U32, name="w_codes", tag="w_codes", align_bytes=64
                    )
                    w_scales[n] = wcode_pool.tile(
                        [P, PASSES, 512], U8, name="w_scales", tag="w_scales", align_bytes=64
                    )
                    w_grouped[n] = grpw_pool.tile(
                        [P, PASSES, HPB, P, 4], BF16, name="w_grouped", tag="w_grouped", align_bytes=64
                    )
                gwords = w_grouped[n][:].bitcast(F32)
                if n == 0:
                    pairs = [(r, 0), (r, 1)]
                    due = [lambda: quantize_w_tile(n, r)]
                else:
                    pairs = [(2 * (r % 2), r // 2), (2 * (r % 2) + 1, r // 2)]
                    due = [lambda: quantize_w_passes(n, r // 2)] if r % 2 == 1 else []
                parts = [
                    (w_raw[n][:, row, :].bitcast(F32), half, gwords[:, 2 * half : 2 * half + 2, row, :, :])
                    for row, half in pairs
                ]
            banks = [transposes(words, half) for words, half, dst in parts]
            if unit[0] == "w" and unit[2] == HPB - 1 and unit[1] + 3 < NT:
                for row in range(HPB):
                    load_w(unit[1] + 3, row)
            for i in range(2):
                dst = parts[i][2]
                src = banks[i][:].rearrange("p (g u r) -> p g r u", g=2, u=2)
                if ((unit[0], i) in vcopy or (unit[0] == "w" and unit[1] >= 2 and unit[2] % 2 == 1 and i == 1)) and not scalar_only:
                    nc.vector.tensor_copy(out=dst, in_=src)
                else:
                    nc.scalar.copy(out=dst, in_=src)
            return due

        gain = keep.tile([P, NH], F32, name="gain", tag="gain")
        kept = {}
        warm_ps = acc_pool.tile([P, 512], F32, name="warm_ps", tag="acc")

        def keep_warm(count):
            for i in range(count):
                nc.tensor.matmul(out=warm_ps[:], lhsT=ones[:], rhs=warm_rhs[:], start=True, stop=True)

        def build_tables(first, last):
            if first == 0:
                cb = tp_pool.tile([P, 512], F32, name="cb", tag="tp")
            else:
                cb = flex_pool.tile([P, 512], F32, name="cb_kept", tag="flex")
                kept["cb"] = cb
            nc.tensor.matmul(out=cb[:, 0:272], lhsT=ones[:], rhs=vec_row[:], start=True, stop=True)
            for which in range(first, last):
                w0 = which * HD
                factor = math.log(S) if which == 0 else 1.0
                tab = keep.tile([P, JT, 2, HD], F32, name="tab%d" % which, tag="tab%d" % which)
                tables[which] = tab
                nc.vector.scalar_tensor_tensor(
                    out=tab[:, :, 0, :],
                    in0=cos_sb[:],
                    scalar=factor,
                    in1=cb[:, w0 : w0 + HD].unsqueeze(1).to_broadcast([P, JT, HD]),
                    op0=MULT,
                    op1=MULT,
                )
                nc.vector.scalar_tensor_tensor(
                    out=tab[:, :, 1, 0:HALF],
                    in0=sin_sb[:, :, HALF:HD],
                    scalar=factor,
                    in1=cb[:, w0 : w0 + HALF].unsqueeze(1).to_broadcast([P, JT, HALF]),
                    op0=MULT,
                    op1=MULT,
                )
                nc.vector.scalar_tensor_tensor(
                    out=tab[:, :, 1, HALF:HD],
                    in0=sin_sb[:, :, 0:HALF],
                    scalar=-factor,
                    in1=cb[:, w0 + HALF : w0 + HD].unsqueeze(1).to_broadcast([P, JT, HALF]),
                    op0=MULT,
                    op1=MULT,
                )
            if first == 0:
                nc.vector.tensor_copy(out=gain[:], in_=cb[:, 2 * HD : 2 * HD + NH])

        def project(acc, n, tt, first, last):
            for g in range(first, last):
                nc.tensor.matmul_mx(
                    out=acc[:],
                    lhsT=x_codes[:, tt, g, :].bitcast(E5X4),
                    lhsT_scale=x_scales[:, tt, g, :],
                    rhs=w_codes[n][:, g, :].bitcast(E5X4),
                    rhs_scale=w_scales[n][:, g, :],
                    start=(g == 0),
                    stop=(g == PASSES - 1),
                )

        def inverse_rms(acc):
            ss = stat_pool.tile([P, HPB], F32, name="ss", tag="ss")
            squares = rope_pool.tile([P, HPB, HD], BF16, name="squares", tag="squares")
            for h in range(HPB):
                nc.scalar.activation(
                    out=squares[:, h, :],
                    in_=acc[:, h * HD : (h + 1) * HD],
                    func=ACT.Square,
                    accum_out=ss[:, h : h + 1],
                )
            root = stat_pool.tile([P, HPB], F32, name="root", tag="root")
            if RSQRT:
                nc.scalar.activation(out=root[:], in_=ss[:], func=ACT.Abs_reciprocal_sqrt, scale=1.0 / HD, bias=EPS)
                return root
            nc.scalar.activation(out=root[:], in_=ss[:], func=ACT.Sqrt, scale=1.0 / HD, bias=EPS)
            rinv = stat_pool.tile([P, HPB], F32, name="rinv", tag="rinv")
            nc.vector.reciprocal(out=rinv[:], in_=root[:])
            return rinv

        def head_factor(n, rinv):
            if n >= NQ:
                return rinv
            rg = stat_pool.tile([P, HPB], F32, name="rg", tag="rg")
            if n == 0:
                nc.gpsimd.tensor_tensor(out=rg[:], in0=rinv[:], in1=gain[:, n * HPB : (n + 1) * HPB], op=MULT)
            else:
                nc.vector.tensor_tensor(
                    out=rg[:], in0=rinv[:], in1=kept["cb"][:, 2 * HD + n * HPB : 2 * HD + (n + 1) * HPB], op=MULT
                )
            return rg

        def rope_head(blk, h):
            nc.vector.scalar_tensor_tensor(
                out=blk["t12"][:, h, :, :],
                in0=blk["acc"][:, h * HD : (h + 1) * HD].unsqueeze(1).to_broadcast([P, 2, HD]),
                scalar=blk["rg"][:, h : h + 1],
                in1=tables[0 if blk["n"] < NQ else 1][:, blk["tt"] % JT, :, :],
                op0=MULT,
                op1=MULT,
            )

        out_tiles = {}

        def finish(blk):
            n, tt = blk["n"], blk["tt"]
            b, j = tt // JT, tt % JT
            if j == 0:
                out_tiles[0] = out_pool.tile([P, HPB, JT, HD], F32, name="o_t", tag="o_t")
            o_t = out_tiles[0]
            t12 = blk["t12"]
            eng = nc.vector if (n == NT - 1 and tt == TT - 1) else nc.gpsimd
            halves = t12[:].rearrange("p h t (u i) -> p h t u i", u=2)
            eng.tensor_tensor(
                out=o_t[:, :, j, :].rearrange("p h (u i) -> p h u i", u=2),
                in0=halves[:, :, 0, :, :],
                in1=halves[:, :, 1, ::-1, :],
                op=ADD,
            )
            if n < NQ:
                dst = out_0[b, n * HPB : (n + 1) * HPB]
            else:
                dst = out_1[b]
            if n == NT - 1 and b == B - 1:
                nc.sync.dma_start(
                    out=dst.rearrange("h (p j) d -> p h j d", j=JT)[:, :, j, :], in_=o_t[:, :, j, :]
                )
            elif j == JT - 1:
                nc.sync.dma_start(
                    out=dst.rearrange("h (p j) d -> p h (j d)", j=JT),
                    in_=o_t[:].rearrange("p h j d -> p h (j d)"),
                )

        head = [("x", 0), ("w", 0, 0), ("w", 0, 1), ("w", 0, 2), ("w", 0, 3), ("x", 1)]
        keep_warm(3)
        for i, unit in enumerate(head):
            for call in prepare(unit):
                call()
            keep_warm(1)
            if i == 0:
                build_tables(0, 1)

        after = units_after()
        between = units_between()
        waiting = []
        prev = None
        older = None
        for m in range(NT * TT):
            n, tt = m // TT, m % TT
            blk = {"n": n, "tt": tt}
            if prev is not None:
                prev["t12"] = rope_pool.tile([P, HPB, 2, HD], F32, name="t12", tag="t12")
                rope_head(prev, 0)
                rope_head(prev, 1)
            if m == TT - 2:
                counts["late"] = 1
            blk["acc"] = result_bank()
            project(blk["acc"], n, tt, 0, PASSES // 2)
            for unit in between.get(m, []):
                waiting.extend(prepare(unit, scalar_only=True))
            project(blk["acc"], n, tt, PASSES // 2, PASSES)
            rinv = inverse_rms(blk["acc"])
            blk["rg"] = head_factor(n, rinv)
            if prev is not None:
                rope_head(prev, 2)
                rope_head(prev, 3)
                if ADD_ON_GPSIMD:
                    finish(prev)
            if older is not None and not ADD_ON_GPSIMD:
                finish(older)
            for call in waiting:
                call()
            waiting = []
            if m == TT - 2:
                build_tables(1, 2)
            for unit in after.get(m, []):
                waiting.extend(prepare(unit))
            older = prev
            prev = blk
        prev["t12"] = rope_pool.tile([P, HPB, 2, HD], F32, name="t12", tag="t12")
        rope_head(prev, 0)
        rope_head(prev, 1)
        if not ADD_ON_GPSIMD:
            finish(older)
        rope_head(prev, 2)
        rope_head(prev, 3)
        finish(prev)
